import numpy as np
import ml_dtypes

BF16 = ml_dtypes.bfloat16


def bf(x):
    return np.asarray(x, np.float32).astype(BF16)


def f32(x):
    return np.asarray(x, np.float32)


def f64(x):
    return np.asarray(x).astype(np.float64)


def striped(idx):
    return np.tile(idx.reshape(-1, 16).T, (8, 1))


C, F, S, N = 1024, 1024, 1024, 128
LN_EPS = 1e-5


def gelu_tanh(v):
    return 0.5 * v * (1.0 + np.tanh(np.sqrt(2.0 / np.pi) * (v + 0.044715 * v**3)))


def setup_inputs():
    return {"base": f32(np.random.standard_normal((C, S))), "hidden": f32(np.random.standard_normal((C, N))), "ln_gain": f32(1.0 + 0.1 * np.random.standard_normal((C, 1))), "ln_bias": f32(0.1 * np.random.standard_normal((C, 1))), "w1": bf(np.random.standard_normal((C, F)) / np.sqrt(C)), "w2": bf(np.random.standard_normal((F, C)) / np.sqrt(F)), "offs": striped(np.random.permutation(S)[:N])}


def reference(base, hidden, ln_gain, ln_bias, w1, w2, offs):
    idx = offs[:16].T.reshape(-1)
    x = f64(hidden)
    mu = x.mean(axis=0, keepdims=True)
    var = ((x - mu) ** 2).mean(axis=0, keepdims=True)
    xn = (x - mu) / np.sqrt(var + LN_EPS) * f64(ln_gain) + f64(ln_bias)
    act = gelu_tanh(f64(w1).T @ xn)
    y = f64(w2).T @ act
    out = f64(base).copy()
    out[:, idx] = x + y
    return out

@@ -1,0 +1,85 @@
+import concourse.mybir as mybir
+
+P = 128
+C, F, S, N = 1024, 1024, 1024, 128
+KB = C // P
+FB = F // P
+LN_EPS = 1e-5
+FLOPS = 2 * N * C * F * 2
+
+F32, BF16, U16 = mybir.dt.float32, mybir.dt.bfloat16, mybir.dt.uint16
+ADD, SUBTRACT, MULT = mybir.AluOpType.add, mybir.AluOpType.subtract, mybir.AluOpType.mult
+ACT = mybir.ActivationFunctionType
+
+
+def tile_hybridattnresidualtransformerblock_kernel(tc, base, hidden, ln_gain, ln_bias, w1, w2, offs, out):
+    nc = tc.nc
+    base_blocks = base.rearrange("(p k) s -> p k s", k=KB)
+    out_blocks = out.rearrange("(p k) s -> p k s", k=KB)
+
+    with (
+        tc.tile_pool(name="held", bufs=1) as held,
+        tc.tile_pool(name="ring", bufs=3) as ring,
+        tc.psum_pool(name="stats", bufs=1) as stats,
+        tc.psum_pool(name="products", bufs=3) as products,
+    ):
+        offsets = held.tile([P, N // 16], U16, name="offsets")
+        nc.sync.dma_start(offsets[:], offs)
+        x = held.tile([P, KB, N], F32, name="x")
+        nc.sync.dma_start(x[:], hidden.rearrange("(p k) j -> p k j", k=KB))
+        gain = held.tile([P, KB], F32, name="gain")
+        nc.sync.dma_start(gain[:], ln_gain.rearrange("(p k) o -> p (k o)", k=KB))
+        bias = held.tile([P, KB], F32, name="bias")
+        nc.sync.dma_start(bias[:], ln_bias.rearrange("(p k) o -> p (k o)", k=KB))
+        w1_sb = held.tile([P, KB, F], BF16, name="w1_sb")
+        nc.sync.dma_start(w1_sb[:], w1.rearrange("(p k) f -> p k f", k=KB))
+        w2_sb = held.tile([P, FB, P, KB], BF16, name="w2_sb")
+        nc.sync.dma_start(w2_sb[:], w2.rearrange("(fb m) (q b) -> m fb q b", m=P, b=KB))
+        windows = [held.tile([P, S], F32, name=f"window{b}") for b in range(KB)]
+        for b in range(KB):
+            nc.sync.dma_start(windows[b][:], base_blocks[:, b, :])
+
+        averager = held.tile([P, P], F32, name="averager")
+        nc.vector.memset(averager[:], 1.0 / C)
+        eps = held.tile([P, 1], F32, name="eps")
+        nc.vector.memset(eps[:], LN_EPS)
+
+        mean = stats.tile([P, N], F32, name="mean")
+        for k in range(KB):
+            nc.tensor.matmul(mean[:], averager[:], x[:, k, :], start=(k == 0), stop=(k == KB - 1))
+        centred = held.tile([P, KB, N], F32, name="centred")
+        squares = held.tile([P, KB, N], F32, name="squares")
+        var = stats.tile([P, N], F32, name="var")
+        for k in range(KB):
+            nc.vector.tensor_tensor(centred[:, k, :], x[:, k, :], mean[:], SUBTRACT)
+            nc.scalar.activation(squares[:, k, :], centred[:, k, :], ACT.Square)
+            nc.tensor.matmul(var[:], averager[:], squares[:, k, :], start=(k == 0), stop=(k == KB - 1))
+        std = held.tile([P, N], F32, name="std")
+        nc.scalar.activation(std[:], var[:], ACT.Sqrt, bias=eps[:])
+        rstd = held.tile([P, N], F32, name="rstd")
+        nc.vector.reciprocal(rstd[:], std[:])
+        normed = held.tile([P, KB, N], F32, name="normed")
+        xn = held.tile([P, KB, N], BF16, name="xn")
+        for k in range(KB):
+            nc.vector.tensor_tensor(normed[:, k, :], centred[:, k, :], rstd[:], MULT)
+            nc.scalar.activation(
+                xn[:, k, :], normed[:, k, :], ACT.Identity, bias=bias[:, k : k + 1], scale=gain[:, k : k + 1]
+            )
+
+        act = held.tile([P, FB, N], BF16, name="act")
+        for fb in range(FB):
+            h = products.tile([P, N], F32, name="h")
+            for k in range(KB):
+                nc.tensor.matmul(
+                    h[:], w1_sb[:, k, fb * P : (fb + 1) * P], xn[:, k, :], start=(k == 0), stop=(k == KB - 1)
+                )
+            nc.scalar.activation(act[:, fb, :], h[:], ACT.Gelu_apprx_tanh)
+
+        for b in range(KB):
+            y = products.tile([P, N], F32, name="y")
+            for fb in range(FB):
+                nc.tensor.matmul(y[:], w2_sb[:, fb, :, b], act[:, fb, :], start=(fb == 0), stop=(fb == FB - 1))
+            y_sb = ring.tile([P, N], F32, name="y_sb")
+            nc.scalar.activation(y_sb[:], y[:], ACT.Copy)
+            nc.vector.tensor_tensor(windows[b][:].indirect(offsets[:]), x[:, b, :], y_sb[:], ADD)
+            nc.sync.dma_start(out_blocks[:, b, :], windows[b][:])

@@ -5,6 +5,7 @@ C, F, S, N = 1024, 1024, 1024, 128
 KB = C // P
 FB = F // P
 LN_EPS = 1e-5
+WARM_UP = 6
 FLOPS = 2 * N * C * F * 2
 
 F32, BF16, U16 = mybir.dt.float32, mybir.dt.bfloat16, mybir.dt.uint16
@@ -20,8 +21,7 @@ def tile_hybridattnresidualtransformerblock_kernel(tc, base, hidden, ln_gain, ln
     with (
         tc.tile_pool(name="held", bufs=1) as held,
         tc.tile_pool(name="ring", bufs=3) as ring,
-        tc.psum_pool(name="stats", bufs=1) as stats,
-        tc.psum_pool(name="products", bufs=3) as products,
+        tc.psum_pool(name="banks", bufs=8) as banks,
     ):
         offsets = held.tile([P, N // 16], U16, name="offsets")
         nc.sync.dma_start(offsets[:], offs)
@@ -43,13 +43,19 @@ def tile_hybridattnresidualtransformerblock_kernel(tc, base, hidden, ln_gain, ln
         nc.vector.memset(averager[:], 1.0 / C)
         eps = held.tile([P, 1], F32, name="eps")
         nc.vector.memset(eps[:], LN_EPS)
+        scratch = held.tile([P, 1], F32, name="scratch")
+        nc.scalar.activation(scratch[:], eps[:], ACT.Sqrt)
 
-        mean = stats.tile([P, N], F32, name="mean")
+        warm = banks.tile([P, P], F32, name="warm", tag="bank")
+        for i in range(WARM_UP):
+            nc.tensor.matmul(warm[:], averager[:], averager[:], start=True, stop=True)
+
+        mean = banks.tile([P, N], F32, name="mean", tag="bank")
         for k in range(KB):
             nc.tensor.matmul(mean[:], averager[:], x[:, k, :], start=(k == 0), stop=(k == KB - 1))
         centred = held.tile([P, KB, N], F32, name="centred")
         squares = held.tile([P, KB, N], F32, name="squares")
-        var = stats.tile([P, N], F32, name="var")
+        var = banks.tile([P, N], F32, name="var", tag="bank")
         for k in range(KB):
             nc.vector.tensor_tensor(centred[:, k, :], x[:, k, :], mean[:], SUBTRACT)
             nc.scalar.activation(squares[:, k, :], centred[:, k, :], ACT.Square)
@@ -60,23 +66,22 @@ def tile_hybridattnresidualtransformerblock_kernel(tc, base, hidden, ln_gain, ln
         nc.vector.reciprocal(rstd[:], std[:])
         normed = held.tile([P, KB, N], F32, name="normed")
         xn = held.tile([P, KB, N], BF16, name="xn")
+        h = [banks.tile([P, N], F32, name=f"h{fb}", tag="bank") for fb in range(FB)]
         for k in range(KB):
             nc.vector.tensor_tensor(normed[:, k, :], centred[:, k, :], rstd[:], MULT)
             nc.scalar.activation(
                 xn[:, k, :], normed[:, k, :], ACT.Identity, bias=bias[:, k : k + 1], scale=gain[:, k : k + 1]
             )
-
+            for fb in range(FB):
+                nc.tensor.matmul(
+                    h[fb][:], w1_sb[:, k, fb * P : (fb + 1) * P], xn[:, k, :], start=(k == 0), stop=(k == KB - 1)
+                )
         act = held.tile([P, FB, N], BF16, name="act")
         for fb in range(FB):
-            h = products.tile([P, N], F32, name="h")
-            for k in range(KB):
-                nc.tensor.matmul(
-                    h[:], w1_sb[:, k, fb * P : (fb + 1) * P], xn[:, k, :], start=(k == 0), stop=(k == KB - 1)
-                )
-            nc.scalar.activation(act[:, fb, :], h[:], ACT.Gelu_apprx_tanh)
+            nc.scalar.activation(act[:, fb, :], h[fb][:], ACT.Gelu_apprx_tanh)
 
         for b in range(KB):
-            y = products.tile([P, N], F32, name="y")
+            y = banks.tile([P, N], F32, name="y", tag="bank")
             for fb in range(FB):
                 nc.tensor.matmul(y[:], w2_sb[:, fb, :, b], act[:, fb, :], start=(fb == 0), stop=(fb == FB - 1))
             y_sb = ring.tile([P, N], F32, name="y_sb")

@@ -5,12 +5,13 @@ C, F, S, N = 1024, 1024, 1024, 128
 KB = C // P
 FB = F // P
 LN_EPS = 1e-5
-WARM_UP = 6
+WARM_UP = 8
 FLOPS = 2 * N * C * F * 2
 
 F32, BF16, U16 = mybir.dt.float32, mybir.dt.bfloat16, mybir.dt.uint16
 ADD, SUBTRACT, MULT = mybir.AluOpType.add, mybir.AluOpType.subtract, mybir.AluOpType.mult
 ACT = mybir.ActivationFunctionType
+AXIS = mybir.AxisListType
 
 
 def tile_hybridattnresidualtransformerblock_kernel(tc, base, hidden, ln_gain, ln_bias, w1, w2, offs, out):
@@ -44,15 +45,16 @@ def tile_hybridattnresidualtransformerblock_kernel(tc, base, hidden, ln_gain, ln
         eps = held.tile([P, 1], F32, name="eps")
         nc.vector.memset(eps[:], LN_EPS)
         scratch = held.tile([P, 1], F32, name="scratch")
-        nc.scalar.activation(scratch[:], eps[:], ACT.Sqrt)
+        nc.scalar.activation(scratch[:], eps[:], ACT.Abs_reciprocal_sqrt)
 
         warm = banks.tile([P, P], F32, name="warm", tag="bank")
         for i in range(WARM_UP):
             nc.tensor.matmul(warm[:], averager[:], averager[:], start=True, stop=True)
 
+        block_sum = held.tile([P, N], F32, name="block_sum")
+        nc.vector.tensor_reduce(block_sum[:], x[:].rearrange("p k j -> p j k"), AXIS.X, ADD)
         mean = banks.tile([P, N], F32, name="mean", tag="bank")
-        for k in range(KB):
-            nc.tensor.matmul(mean[:], averager[:], x[:, k, :], start=(k == 0), stop=(k == KB - 1))
+        nc.tensor.matmul(mean[:], averager[:], block_sum[:], start=True, stop=True)
         centred = held.tile([P, KB, N], F32, name="centred")
         squares = held.tile([P, KB, N], F32, name="squares")
         var = banks.tile([P, N], F32, name="var", tag="bank")
@@ -60,10 +62,8 @@ def tile_hybridattnresidualtransformerblock_kernel(tc, base, hidden, ln_gain, ln
             nc.vector.tensor_tensor(centred[:, k, :], x[:, k, :], mean[:], SUBTRACT)
             nc.scalar.activation(squares[:, k, :], centred[:, k, :], ACT.Square)
             nc.tensor.matmul(var[:], averager[:], squares[:, k, :], start=(k == 0), stop=(k == KB - 1))
-        std = held.tile([P, N], F32, name="std")
-        nc.scalar.activation(std[:], var[:], ACT.Sqrt, bias=eps[:])
         rstd = held.tile([P, N], F32, name="rstd")
-        nc.vector.reciprocal(rstd[:], std[:])
+        nc.scalar.activation(rstd[:], var[:], ACT.Abs_reciprocal_sqrt, bias=eps[:])
         normed = held.tile([P, KB, N], F32, name="normed")
         xn = held.tile([P, KB, N], BF16, name="xn")
         h = [banks.tile([P, N], F32, name=f"h{fb}", tag="bank") for fb in range(FB)]

@@ -32,10 +32,10 @@ def tile_hybridattnresidualtransformerblock_kernel(tc, base, hidden, ln_gain, ln
         nc.sync.dma_start(gain[:], ln_gain.rearrange("(p k) o -> p (k o)", k=KB))
         bias = held.tile([P, KB], F32, name="bias")
         nc.sync.dma_start(bias[:], ln_bias.rearrange("(p k) o -> p (k o)", k=KB))
-        w1_sb = held.tile([P, KB, F], BF16, name="w1_sb")
-        nc.sync.dma_start(w1_sb[:], w1.rearrange("(p k) f -> p k f", k=KB))
+        w1_sb = held.tile([P, KB, P, FB], BF16, name="w1_sb")
+        nc.sync.dma_start(w1_sb[:], w1.rearrange("(p k) (m fb) -> p k m fb", k=KB, fb=FB))
         w2_sb = held.tile([P, FB, P, KB], BF16, name="w2_sb")
-        nc.sync.dma_start(w2_sb[:], w2.rearrange("(fb m) (q b) -> m fb q b", m=P, b=KB))
+        nc.sync.dma_start(w2_sb[:], w2.rearrange("(m fb) (q b) -> m fb q b", fb=FB, b=KB))
         windows = [held.tile([P, S], F32, name=f"window{b}") for b in range(KB)]
         for b in range(KB):
             nc.sync.dma_start(windows[b][:], base_blocks[:, b, :])
@@ -73,9 +73,7 @@ def tile_hybridattnresidualtransformerblock_kernel(tc, base, hidden, ln_gain, ln
                 xn[:, k, :], normed[:, k, :], ACT.Identity, bias=bias[:, k : k + 1], scale=gain[:, k : k + 1]
             )
             for fb in range(FB):
-                nc.tensor.matmul(
-                    h[fb][:], w1_sb[:, k, fb * P : (fb + 1) * P], xn[:, k, :], start=(k == 0), stop=(k == KB - 1)
-                )
+                nc.tensor.matmul(h[fb][:], w1_sb[:, k, :, fb], xn[:, k, :], start=(k == 0), stop=(k == KB - 1))
         act = held.tile([P, FB, N], BF16, name="act")
         for fb in range(FB):
             nc.scalar.activation(act[:, fb, :], h[fb][:], ACT.Gelu_apprx_tanh)

@@ -5,8 +5,7 @@ C, F, S, N = 1024, 1024, 1024, 128
 KB = C // P
 FB = F // P
 LN_EPS = 1e-5
-WARM_UP = 8
-FLOPS = 2 * N * C * F * 2
+FLOPS = 2 * (2 * C * F * N)
 
 F32, BF16, U16 = mybir.dt.float32, mybir.dt.bfloat16, mybir.dt.uint16
 ADD, SUBTRACT, MULT = mybir.AluOpType.add, mybir.AluOpType.subtract, mybir.AluOpType.mult
@@ -21,8 +20,9 @@ def tile_hybridattnresidualtransformerblock_kernel(tc, base, hidden, ln_gain, ln
 
     with (
         tc.tile_pool(name="held", bufs=1) as held,
-        tc.tile_pool(name="ring", bufs=3) as ring,
-        tc.psum_pool(name="banks", bufs=8) as banks,
+        tc.tile_pool(name="ring", bufs=2) as ring,
+        tc.psum_pool(name="stats", bufs=1) as stats,
+        tc.psum_pool(name="products", bufs=2) as products,
     ):
         offsets = held.tile([P, N // 16], U16, name="offsets")
         nc.sync.dma_start(offsets[:], offs)
@@ -44,20 +44,14 @@ def tile_hybridattnresidualtransformerblock_kernel(tc, base, hidden, ln_gain, ln
         nc.vector.memset(averager[:], 1.0 / C)
         eps = held.tile([P, 1], F32, name="eps")
         nc.vector.memset(eps[:], LN_EPS)
-        scratch = held.tile([P, 1], F32, name="scratch")
-        nc.scalar.activation(scratch[:], eps[:], ACT.Abs_reciprocal_sqrt)
-
-        warm = banks.tile([P, P], F32, name="warm", tag="bank")
-        for i in range(WARM_UP):
-            nc.tensor.matmul(warm[:], averager[:], averager[:], start=True, stop=True)
 
         block_sum = held.tile([P, N], F32, name="block_sum")
         nc.vector.tensor_reduce(block_sum[:], x[:].rearrange("p k j -> p j k"), AXIS.X, ADD)
-        mean = banks.tile([P, N], F32, name="mean", tag="bank")
+        mean = stats.tile([P, N], F32, name="mean")
         nc.tensor.matmul(mean[:], averager[:], block_sum[:], start=True, stop=True)
         centred = held.tile([P, KB, N], F32, name="centred")
         squares = held.tile([P, KB, N], F32, name="squares")
-        var = banks.tile([P, N], F32, name="var", tag="bank")
+        var = stats.tile([P, N], F32, name="var")
         for k in range(KB):
             nc.vector.tensor_tensor(centred[:, k, :], x[:, k, :], mean[:], SUBTRACT)
             nc.scalar.activation(squares[:, k, :], centred[:, k, :], ACT.Square)
@@ -66,20 +60,21 @@ def tile_hybridattnresidualtransformerblock_kernel(tc, base, hidden, ln_gain, ln
         nc.scalar.activation(rstd[:], var[:], ACT.Abs_reciprocal_sqrt, bias=eps[:])
         normed = held.tile([P, KB, N], F32, name="normed")
         xn = held.tile([P, KB, N], BF16, name="xn")
-        h = [banks.tile([P, N], F32, name=f"h{fb}", tag="bank") for fb in range(FB)]
         for k in range(KB):
             nc.vector.tensor_tensor(normed[:, k, :], centred[:, k, :], rstd[:], MULT)
             nc.scalar.activation(
                 xn[:, k, :], normed[:, k, :], ACT.Identity, bias=bias[:, k : k + 1], scale=gain[:, k : k + 1]
             )
-            for fb in range(FB):
-                nc.tensor.matmul(h[fb][:], w1_sb[:, k, :, fb], xn[:, k, :], start=(k == 0), stop=(k == KB - 1))
+
         act = held.tile([P, FB, N], BF16, name="act")
         for fb in range(FB):
-            nc.scalar.activation(act[:, fb, :], h[fb][:], ACT.Gelu_apprx_tanh)
+            h = products.tile([P, N], F32, name="h")
+            for k in range(KB):
+                nc.tensor.matmul(h[:], w1_sb[:, k, :, fb], xn[:, k, :], start=(k == 0), stop=(k == KB - 1))
+            nc.scalar.activation(act[:, fb, :], h[:], ACT.Gelu_apprx_tanh)
 
         for b in range(KB):
-            y = banks.tile([P, N], F32, name="y", tag="bank")
+            y = products.tile([P, N], F32, name="y")
             for fb in range(FB):
                 nc.tensor.matmul(y[:], w2_sb[:, fb, :, b], act[:, fb, :], start=(fb == 0), stop=(fb == FB - 1))
             y_sb = ring.tile([P, N], F32, name="y_sb")

@@ -4,7 +4,9 @@ P = 128
 C, F, S, N = 1024, 1024, 1024, 128
 KB = C // P
 FB = F // P
+PSUM_BANKS = 8
 LN_EPS = 1e-5
+WARM_UP = 8
 FLOPS = 2 * (2 * C * F * N)
 
 F32, BF16, U16 = mybir.dt.float32, mybir.dt.bfloat16, mybir.dt.uint16
@@ -20,9 +22,8 @@ def tile_hybridattnresidualtransformerblock_kernel(tc, base, hidden, ln_gain, ln
 
     with (
         tc.tile_pool(name="held", bufs=1) as held,
-        tc.tile_pool(name="ring", bufs=2) as ring,
-        tc.psum_pool(name="stats", bufs=1) as stats,
-        tc.psum_pool(name="products", bufs=2) as products,
+        tc.tile_pool(name="ring", bufs=3) as ring,
+        tc.psum_pool(name="banks", bufs=PSUM_BANKS) as banks,
     ):
         offsets = held.tile([P, N // 16], U16, name="offsets")
         nc.sync.dma_start(offsets[:], offs)
@@ -45,36 +46,40 @@ def tile_hybridattnresidualtransformerblock_kernel(tc, base, hidden, ln_gain, ln
         eps = held.tile([P, 1], F32, name="eps")
         nc.vector.memset(eps[:], LN_EPS)
 
+        warm = banks.tile([P, P], F32, name="warm", tag="bank")
+        for i in range(WARM_UP):
+            nc.tensor.matmul(warm[:], averager[:], averager[:], start=True, stop=True)
+
         block_sum = held.tile([P, N], F32, name="block_sum")
         nc.vector.tensor_reduce(block_sum[:], x[:].rearrange("p k j -> p j k"), AXIS.X, ADD)
-        mean = stats.tile([P, N], F32, name="mean")
+        mean = banks.tile([P, N], F32, name="mean", tag="bank")
         nc.tensor.matmul(mean[:], averager[:], block_sum[:], start=True, stop=True)
         centred = held.tile([P, KB, N], F32, name="centred")
         squares = held.tile([P, KB, N], F32, name="squares")
-        var = stats.tile([P, N], F32, name="var")
+        var = banks.tile([P, N], F32, name="var", tag="bank")
         for k in range(KB):
             nc.vector.tensor_tensor(centred[:, k, :], x[:, k, :], mean[:], SUBTRACT)
             nc.scalar.activation(squares[:, k, :], centred[:, k, :], ACT.Square)
             nc.tensor.matmul(var[:], averager[:], squares[:, k, :], start=(k == 0), stop=(k == KB - 1))
         rstd = held.tile([P, N], F32, name="rstd")
         nc.scalar.activation(rstd[:], var[:], ACT.Abs_reciprocal_sqrt, bias=eps[:])
+
         normed = held.tile([P, KB, N], F32, name="normed")
         xn = held.tile([P, KB, N], BF16, name="xn")
+        h = [banks.tile([P, N], F32, name=f"h{fb}", tag="bank") for fb in range(FB)]
         for k in range(KB):
             nc.vector.tensor_tensor(normed[:, k, :], centred[:, k, :], rstd[:], MULT)
             nc.scalar.activation(
                 xn[:, k, :], normed[:, k, :], ACT.Identity, bias=bias[:, k : k + 1], scale=gain[:, k : k + 1]
             )
-
+            for fb in range(FB):
+                nc.tensor.matmul(h[fb][:], w1_sb[:, k, :, fb], xn[:, k, :], start=(k == 0), stop=(k == KB - 1))
         act = held.tile([P, FB, N], BF16, name="act")
         for fb in range(FB):
-            h = products.tile([P, N], F32, name="h")
-            for k in range(KB):
-                nc.tensor.matmul(h[:], w1_sb[:, k, :, fb], xn[:, k, :], start=(k == 0), stop=(k == KB - 1))
-            nc.scalar.activation(act[:, fb, :], h[:], ACT.Gelu_apprx_tanh)
+            nc.scalar.activation(act[:, fb, :], h[fb][:], ACT.Gelu_apprx_tanh)
 
         for b in range(KB):
-            y = products.tile([P, N], F32, name="y")
+            y = banks.tile([P, N], F32, name="y", tag="bank")
             for fb in range(FB):
                 nc.tensor.matmul(y[:], w2_sb[:, fb, :, b], act[:, fb, :], start=(fb == 0), stop=(fb == FB - 1))
             y_sb = ring.tile([P, N], F32, name="y_sb")

@@ -85,4 +85,4 @@ def tile_hybridattnresidualtransformerblock_kernel(tc, base, hidden, ln_gain, ln
             y_sb = ring.tile([P, N], F32, name="y_sb")
             nc.scalar.activation(y_sb[:], y[:], ACT.Copy)
             nc.vector.tensor_tensor(windows[b][:].indirect(offsets[:]), x[:, b, :], y_sb[:], ADD)
-            nc.sync.dma_start(out_blocks[:, b, :], windows[b][:])
+            (nc.sync, nc.scalar)[b % 2].dma_start(out_blocks[:, b, :], windows[b][:])

@@ -6,7 +6,6 @@ KB = C // P
 FB = F // P
 PSUM_BANKS = 8
 LN_EPS = 1e-5
-WARM_UP = 8
 FLOPS = 2 * (2 * C * F * N)
 
 F32, BF16, U16 = mybir.dt.float32, mybir.dt.bfloat16, mybir.dt.uint16
@@ -46,10 +45,6 @@ def tile_hybridattnresidualtransformerblock_kernel(tc, base, hidden, ln_gain, ln
         eps = held.tile([P, 1], F32, name="eps")
         nc.vector.memset(eps[:], LN_EPS)
 
-        warm = banks.tile([P, P], F32, name="warm", tag="bank")
-        for i in range(WARM_UP):
-            nc.tensor.matmul(warm[:], averager[:], averager[:], start=True, stop=True)
-
         block_sum = held.tile([P, N], F32, name="block_sum")
         nc.vector.tensor_reduce(block_sum[:], x[:].rearrange("p k j -> p j k"), AXIS.X, ADD)
         mean = banks.tile([P, N], F32, name="mean", tag="bank")
@@ -85,4 +80,4 @@ def tile_hybridattnresidualtransformerblock_kernel(tc, base, hidden, ln_gain, ln
             y_sb = ring.tile([P, N], F32, name="y_sb")
             nc.scalar.activation(y_sb[:], y[:], ACT.Copy)
             nc.vector.tensor_tensor(windows[b][:].indirect(offsets[:]), x[:, b, :], y_sb[:], ADD)
-            (nc.sync, nc.scalar)[b % 2].dma_start(out_blocks[:, b, :], windows[b][:])
+            nc.sync.dma_start(out_blocks[:, b, :], windows[b][:])

@@ -4,6 +4,7 @@ P = 128
 C, F, S, N = 1024, 1024, 1024, 128
 KB = C // P
 FB = F // P
+PAIRS = KB // 2
 PSUM_BANKS = 8
 LN_EPS = 1e-5
 FLOPS = 2 * (2 * C * F * N)
@@ -11,7 +12,6 @@ FLOPS = 2 * (2 * C * F * N)
 F32, BF16, U16 = mybir.dt.float32, mybir.dt.bfloat16, mybir.dt.uint16
 ADD, SUBTRACT, MULT = mybir.AluOpType.add, mybir.AluOpType.subtract, mybir.AluOpType.mult
 ACT = mybir.ActivationFunctionType
-AXIS = mybir.AxisListType
 
 
 def tile_hybridattnresidualtransformerblock_kernel(tc, base, hidden, ln_gain, ln_bias, w1, w2, offs, out):
@@ -45,32 +45,52 @@ def tile_hybridattnresidualtransformerblock_kernel(tc, base, hidden, ln_gain, ln
         eps = held.tile([P, 1], F32, name="eps")
         nc.vector.memset(eps[:], LN_EPS)
 
-        block_sum = held.tile([P, N], F32, name="block_sum")
-        nc.vector.tensor_reduce(block_sum[:], x[:].rearrange("p k j -> p j k"), AXIS.X, ADD)
+        warm = held.tile([P, 1], F32, name="warm")
+        nc.scalar.activation(warm[:], eps[:], ACT.Abs_reciprocal_sqrt)
+
+        sum4 = held.tile([P, 4, N], F32, name="sum4")
+        nc.vector.tensor_tensor(sum4[:], x[:, 0:4, :], x[:, 4:8, :], ADD)
+        sum2 = held.tile([P, 2, N], F32, name="sum2")
+        nc.vector.tensor_tensor(sum2[:], sum4[:, 0:2, :], sum4[:, 2:4, :], ADD)
+        sum1 = held.tile([P, N], F32, name="sum1")
+        nc.vector.tensor_tensor(sum1[:], sum2[:, 0, :], sum2[:, 1, :], ADD)
         mean = banks.tile([P, N], F32, name="mean", tag="bank")
-        nc.tensor.matmul(mean[:], averager[:], block_sum[:], start=True, stop=True)
+        nc.tensor.matmul(mean[:], averager[:], sum1[:], start=True, stop=True)
         centred = held.tile([P, KB, N], F32, name="centred")
         squares = held.tile([P, KB, N], F32, name="squares")
+        pair_sums = held.tile([P, PAIRS, N], F32, name="pair_sums")
         var = banks.tile([P, N], F32, name="var", tag="bank")
-        for k in range(KB):
-            nc.vector.tensor_tensor(centred[:, k, :], x[:, k, :], mean[:], SUBTRACT)
-            nc.scalar.activation(squares[:, k, :], centred[:, k, :], ACT.Square)
-            nc.tensor.matmul(var[:], averager[:], squares[:, k, :], start=(k == 0), stop=(k == KB - 1))
+        mean_twice = mean[:].unsqueeze(1).to_broadcast([P, 2, N])
+        for i in range(PAIRS):
+            pair = slice(2 * i, 2 * i + 2)
+            nc.vector.tensor_tensor(centred[:, pair, :], x[:, pair, :], mean_twice, SUBTRACT)
+            nc.scalar.activation(squares[:, pair, :], centred[:, pair, :], ACT.Square)
+        for i in range(PAIRS):
+            nc.vector.tensor_tensor(pair_sums[:, i, :], squares[:, 2 * i, :], squares[:, 2 * i + 1, :], ADD)
+            nc.tensor.matmul(var[:], averager[:], pair_sums[:, i, :], start=(i == 0), stop=(i == PAIRS - 1))
         rstd = held.tile([P, N], F32, name="rstd")
         nc.scalar.activation(rstd[:], var[:], ACT.Abs_reciprocal_sqrt, bias=eps[:])
 
         normed = held.tile([P, KB, N], F32, name="normed")
         xn = held.tile([P, KB, N], BF16, name="xn")
+        rstd_twice = rstd[:].unsqueeze(1).to_broadcast([P, 2, N])
+        for i in range(PAIRS):
+            pair = slice(2 * i, 2 * i + 2)
+            nc.vector.tensor_tensor(normed[:, pair, :], centred[:, pair, :], rstd_twice, MULT)
+            for k in range(2 * i, 2 * i + 2):
+                nc.scalar.activation(
+                    xn[:, k, :], normed[:, k, :], ACT.Identity, bias=bias[:, k : k + 1], scale=gain[:, k : k + 1]
+                )
+        act = held.tile([P, FB, N], BF16, name="act")
         h = [banks.tile([P, N], F32, name=f"h{fb}", tag="bank") for fb in range(FB)]
         for k in range(KB):
-            nc.vector.tensor_tensor(normed[:, k, :], centred[:, k, :], rstd[:], MULT)
-            nc.scalar.activation(
-                xn[:, k, :], normed[:, k, :], ACT.Identity, bias=bias[:, k : k + 1], scale=gain[:, k : k + 1]
-            )
-            for fb in range(FB):
+            for fb in range(FB // 2):
                 nc.tensor.matmul(h[fb][:], w1_sb[:, k, :, fb], xn[:, k, :], start=(k == 0), stop=(k == KB - 1))
-        act = held.tile([P, FB, N], BF16, name="act")
-        for fb in range(FB):
+        for fb in range(FB // 2):
+            nc.scalar.activation(act[:, fb, :], h[fb][:], ACT.Gelu_apprx_tanh)
+        for fb in range(FB // 2, FB):
+            for k in range(KB):
+                nc.tensor.matmul(h[fb][:], w1_sb[:, k, :, fb], xn[:, k, :], start=(k == 0), stop=(k == KB - 1))
             nc.scalar.activation(act[:, fb, :], h[fb][:], ACT.Gelu_apprx_tanh)
 
         for b in range(KB):

@@ -5,6 +5,7 @@ C, F, S, N = 1024, 1024, 1024, 128
 KB = C // P
 FB = F // P
 PAIRS = KB // 2
+SLAB = KB // 2
 PSUM_BANKS = 8
 LN_EPS = 1e-5
 FLOPS = 2 * (2 * C * F * N)
@@ -34,11 +35,12 @@ def tile_hybridattnresidualtransformerblock_kernel(tc, base, hidden, ln_gain, ln
         nc.sync.dma_start(bias[:], ln_bias.rearrange("(p k) o -> p (k o)", k=KB))
         w1_sb = held.tile([P, KB, P, FB], BF16, name="w1_sb")
         nc.sync.dma_start(w1_sb[:], w1.rearrange("(p k) (m fb) -> p k m fb", k=KB, fb=FB))
+        slabs = [held.tile([P, SLAB, S], F32, name=f"slab{i}") for i in range(KB // SLAB)]
+        nc.sync.dma_start(slabs[0][:], base_blocks[:, 0:SLAB, :])
         w2_sb = held.tile([P, FB, P, KB], BF16, name="w2_sb")
         nc.sync.dma_start(w2_sb[:], w2.rearrange("(m fb) (q b) -> m fb q b", fb=FB, b=KB))
+        nc.sync.dma_start(slabs[1][:], base_blocks[:, SLAB:KB, :])
         windows = [held.tile([P, S], F32, name=f"window{b}") for b in range(KB)]
-        for b in range(KB):
-            nc.sync.dma_start(windows[b][:], base_blocks[:, b, :])
 
         averager = held.tile([P, P], F32, name="averager")
         nc.vector.memset(averager[:], 1.0 / C)
@@ -81,6 +83,8 @@ def tile_hybridattnresidualtransformerblock_kernel(tc, base, hidden, ln_gain, ln
                 nc.scalar.activation(
                     xn[:, k, :], normed[:, k, :], ACT.Identity, bias=bias[:, k : k + 1], scale=gain[:, k : k + 1]
                 )
+        for b in range(SLAB):
+            nc.vector.tensor_copy(windows[b][:], slabs[0][:, b, :])
         act = held.tile([P, FB, N], BF16, name="act")
         h = [banks.tile([P, N], F32, name=f"h{fb}", tag="bank") for fb in range(FB)]
         for k in range(KB):
@@ -99,5 +103,7 @@ def tile_hybridattnresidualtransformerblock_kernel(tc, base, hidden, ln_gain, ln
                 nc.tensor.matmul(y[:], w2_sb[:, fb, :, b], act[:, fb, :], start=(fb == 0), stop=(fb == FB - 1))
             y_sb = ring.tile([P, N], F32, name="y_sb")
             nc.scalar.activation(y_sb[:], y[:], ACT.Copy)
+            if b < SLAB:
+                nc.scalar.activation(windows[SLAB + b][:], slabs[1][:, b, :], ACT.Copy)
             nc.vector.tensor_tensor(windows[b][:].indirect(offsets[:]), x[:, b, :], y_sb[:], ADD)
             nc.sync.dma_start(out_blocks[:, b, :], windows[b][:])

@@ -22,11 +22,9 @@ def tile_hybridattnresidualtransformerblock_kernel(tc, base, hidden, ln_gain, ln
 
     with (
         tc.tile_pool(name="held", bufs=1) as held,
-        tc.tile_pool(name="ring", bufs=3) as ring,
+        tc.tile_pool(name="ring", bufs=KB) as ring,
         tc.psum_pool(name="banks", bufs=PSUM_BANKS) as banks,
     ):
-        offsets = held.tile([P, N // 16], U16, name="offsets")
-        nc.sync.dma_start(offsets[:], offs)
         x = held.tile([P, KB, N], F32, name="x")
         nc.sync.dma_start(x[:], hidden.rearrange("(p k) j -> p k j", k=KB))
         gain = held.tile([P, KB], F32, name="gain")
@@ -39,6 +37,8 @@ def tile_hybridattnresidualtransformerblock_kernel(tc, base, hidden, ln_gain, ln
         nc.sync.dma_start(slabs[0][:], base_blocks[:, 0:SLAB, :])
         w2_sb = held.tile([P, FB, P, KB], BF16, name="w2_sb")
         nc.sync.dma_start(w2_sb[:], w2.rearrange("(m fb) (q b) -> m fb q b", fb=FB, b=KB))
+        offsets = held.tile([P, N // 16], U16, name="offsets")
+        nc.sync.dma_start(offsets[:], offs)
         nc.sync.dma_start(slabs[1][:], base_blocks[:, SLAB:KB, :])
         windows = [held.tile([P, S], F32, name=f"window{b}") for b in range(KB)]
 
@@ -67,7 +67,6 @@ def tile_hybridattnresidualtransformerblock_kernel(tc, base, hidden, ln_gain, ln
             pair = slice(2 * i, 2 * i + 2)
             nc.vector.tensor_tensor(centred[:, pair, :], x[:, pair, :], mean_twice, SUBTRACT)
             nc.scalar.activation(squares[:, pair, :], centred[:, pair, :], ACT.Square)
-        for i in range(PAIRS):
             nc.vector.tensor_tensor(pair_sums[:, i, :], squares[:, 2 * i, :], squares[:, 2 * i + 1, :], ADD)
             nc.tensor.matmul(var[:], averager[:], pair_sums[:, i, :], start=(i == 0), stop=(i == PAIRS - 1))
         rstd = held.tile([P, N], F32, name="rstd")
@@ -103,7 +102,11 @@ def tile_hybridattnresidualtransformerblock_kernel(tc, base, hidden, ln_gain, ln
                 nc.tensor.matmul(y[:], w2_sb[:, fb, :, b], act[:, fb, :], start=(fb == 0), stop=(fb == FB - 1))
             y_sb = ring.tile([P, N], F32, name="y_sb")
             nc.scalar.activation(y_sb[:], y[:], ACT.Copy)
-            if b < SLAB:
-                nc.scalar.activation(windows[SLAB + b][:], slabs[1][:, b, :], ACT.Copy)
             nc.vector.tensor_tensor(windows[b][:].indirect(offsets[:]), x[:, b, :], y_sb[:], ADD)
             nc.sync.dma_start(out_blocks[:, b, :], windows[b][:])
+            if b == 1 or b == 3:
+                fill = SLAB + b // 2
+                nc.vector.tensor_copy(windows[fill][:], slabs[1][:, fill - SLAB, :])
+            if b == SLAB - 1:
+                for fill in range(SLAB + 2, KB):
+                    nc.scalar.activation(windows[fill][:], slabs[1][:, fill - SLAB, :], ACT.Copy)

@@ -31,14 +31,14 @@ def tile_hybridattnresidualtransformerblock_kernel(tc, base, hidden, ln_gain, ln
         nc.sync.dma_start(gain[:], ln_gain.rearrange("(p k) o -> p (k o)", k=KB))
         bias = held.tile([P, KB], F32, name="bias")
         nc.sync.dma_start(bias[:], ln_bias.rearrange("(p k) o -> p (k o)", k=KB))
+        offsets = held.tile([P, N // 16], U16, name="offsets")
+        nc.sync.dma_start(offsets[:], offs)
         w1_sb = held.tile([P, KB, P, FB], BF16, name="w1_sb")
         nc.sync.dma_start(w1_sb[:], w1.rearrange("(p k) (m fb) -> p k m fb", k=KB, fb=FB))
         slabs = [held.tile([P, SLAB, S], F32, name=f"slab{i}") for i in range(KB // SLAB)]
         nc.sync.dma_start(slabs[0][:], base_blocks[:, 0:SLAB, :])
         w2_sb = held.tile([P, FB, P, KB], BF16, name="w2_sb")
         nc.sync.dma_start(w2_sb[:], w2.rearrange("(m fb) (q b) -> m fb q b", fb=FB, b=KB))
-        offsets = held.tile([P, N // 16], U16, name="offsets")
-        nc.sync.dma_start(offsets[:], offs)
         nc.sync.dma_start(slabs[1][:], base_blocks[:, SLAB:KB, :])
         windows = [held.tile([P, S], F32, name=f"window{b}") for b in range(KB)]
 
@@ -50,25 +50,21 @@ def tile_hybridattnresidualtransformerblock_kernel(tc, base, hidden, ln_gain, ln
         warm = held.tile([P, 1], F32, name="warm")
         nc.scalar.activation(warm[:], eps[:], ACT.Abs_reciprocal_sqrt)
 
-        sum4 = held.tile([P, 4, N], F32, name="sum4")
-        nc.vector.tensor_tensor(sum4[:], x[:, 0:4, :], x[:, 4:8, :], ADD)
-        sum2 = held.tile([P, 2, N], F32, name="sum2")
-        nc.vector.tensor_tensor(sum2[:], sum4[:, 0:2, :], sum4[:, 2:4, :], ADD)
-        sum1 = held.tile([P, N], F32, name="sum1")
-        nc.vector.tensor_tensor(sum1[:], sum2[:, 0, :], sum2[:, 1, :], ADD)
+        sum4 = held.tile([P, KB // 2, N], F32, name="sum4")
+        nc.vector.tensor_tensor(sum4[:], x[:, 0 : KB // 2, :], x[:, KB // 2 : KB, :], ADD)
         mean = banks.tile([P, N], F32, name="mean", tag="bank")
-        nc.tensor.matmul(mean[:], averager[:], sum1[:], start=True, stop=True)
+        for i in range(KB // 2):
+            nc.tensor.matmul(mean[:], averager[:], sum4[:, i, :], start=(i == 0), stop=(i == KB // 2 - 1))
         centred = held.tile([P, KB, N], F32, name="centred")
         squares = held.tile([P, KB, N], F32, name="squares")
-        pair_sums = held.tile([P, PAIRS, N], F32, name="pair_sums")
         var = banks.tile([P, N], F32, name="var", tag="bank")
         mean_twice = mean[:].unsqueeze(1).to_broadcast([P, 2, N])
         for i in range(PAIRS):
             pair = slice(2 * i, 2 * i + 2)
             nc.vector.tensor_tensor(centred[:, pair, :], x[:, pair, :], mean_twice, SUBTRACT)
             nc.scalar.activation(squares[:, pair, :], centred[:, pair, :], ACT.Square)
-            nc.vector.tensor_tensor(pair_sums[:, i, :], squares[:, 2 * i, :], squares[:, 2 * i + 1, :], ADD)
-            nc.tensor.matmul(var[:], averager[:], pair_sums[:, i, :], start=(i == 0), stop=(i == PAIRS - 1))
+            for k in range(2 * i, 2 * i + 2):
+                nc.tensor.matmul(var[:], averager[:], squares[:, k, :], start=(k == 0), stop=(k == KB - 1))
         rstd = held.tile([P, N], F32, name="rstd")
         nc.scalar.activation(rstd[:], var[:], ACT.Abs_reciprocal_sqrt, bias=eps[:])
 

@@ -5,6 +5,7 @@ C, F, S, N = 1024, 1024, 1024, 128
 KB = C // P
 FB = F // P
 PAIRS = KB // 2
+ROWS = 32
 SLAB = KB // 2
 PSUM_BANKS = 8
 LN_EPS = 1e-5
@@ -27,10 +28,9 @@ def tile_hybridattnresidualtransformerblock_kernel(tc, base, hidden, ln_gain, ln
     ):
         x = held.tile([P, KB, N], F32, name="x")
         nc.sync.dma_start(x[:], hidden.rearrange("(p k) j -> p k j", k=KB))
-        gain = held.tile([P, KB], F32, name="gain")
-        nc.sync.dma_start(gain[:], ln_gain.rearrange("(p k) o -> p (k o)", k=KB))
-        bias = held.tile([P, KB], F32, name="bias")
-        nc.sync.dma_start(bias[:], ln_bias.rearrange("(p k) o -> p (k o)", k=KB))
+        gain_bias_rows = held.tile([ROWS, 2, ROWS], F32, name="gain_bias_rows")
+        nc.sync.dma_start(gain_bias_rows[:, 0, :], ln_gain.rearrange("(r i) o -> r (i o)", r=ROWS))
+        nc.sync.dma_start(gain_bias_rows[:, 1, :], ln_bias.rearrange("(r i) o -> r (i o)", r=ROWS))
         offsets = held.tile([P, N // 16], U16, name="offsets")
         nc.sync.dma_start(offsets[:], offs)
         w1_sb = held.tile([P, KB, P, FB], BF16, name="w1_sb")
@@ -47,6 +47,18 @@ def tile_hybridattnresidualtransformerblock_kernel(tc, base, hidden, ln_gain, ln
         eps = held.tile([P, 1], F32, name="eps")
         nc.vector.memset(eps[:], LN_EPS)
 
+        pick = held.tile([ROWS, P // ROWS, P], F32, name="pick")
+        nc.gpsimd.memset(pick[:], 0.0)
+        nc.gpsimd.affine_select(
+            out=pick[:],
+            in_=pick[:],
+            compare_op=mybir.AluOpType.not_equal,
+            fill=1.0,
+            base=0,
+            pattern=[[1, P // ROWS], [-1, P]],
+            channel_multiplier=P // ROWS,
+        )
+
         warm = held.tile([P, 1], F32, name="warm")
         nc.scalar.activation(warm[:], eps[:], ACT.Abs_reciprocal_sqrt)
 
@@ -55,6 +67,12 @@ def tile_hybridattnresidualtransformerblock_kernel(tc, base, hidden, ln_gain, ln
         mean = banks.tile([P, N], F32, name="mean", tag="bank")
         for i in range(KB // 2):
             nc.tensor.matmul(mean[:], averager[:], sum4[:, i, :], start=(i == 0), stop=(i == KB // 2 - 1))
+        spread = banks.tile([P, 2, KB], F32, name="spread", tag="bank")
+        for a in range(P // ROWS):
+            eight = gain_bias_rows[:, :, KB * a : KB * (a + 1)]
+            nc.tensor.matmul(spread[:], pick[:, a, :], eight, start=(a == 0), stop=(a == P // ROWS - 1))
+        gain_bias = held.tile([P, 2, KB], F32, name="gain_bias")
+        nc.vector.tensor_copy(gain_bias[:], spread[:])
         centred = held.tile([P, KB, N], F32, name="centred")
         squares = held.tile([P, KB, N], F32, name="squares")
         var = banks.tile([P, N], F32, name="var", tag="bank")
@@ -76,7 +94,11 @@ def tile_hybridattnresidualtransformerblock_kernel(tc, base, hidden, ln_gain, ln
             nc.vector.tensor_tensor(normed[:, pair, :], centred[:, pair, :], rstd_twice, MULT)
             for k in range(2 * i, 2 * i + 2):
                 nc.scalar.activation(
-                    xn[:, k, :], normed[:, k, :], ACT.Identity, bias=bias[:, k : k + 1], scale=gain[:, k : k + 1]
+                    xn[:, k, :],
+                    normed[:, k, :],
+                    ACT.Identity,
+                    bias=gain_bias[:, 1, k : k + 1],
+                    scale=gain_bias[:, 0, k : k + 1],
                 )
         for b in range(SLAB):
             nc.vector.tensor_copy(windows[b][:], slabs[0][:, b, :])

@@ -122,9 +122,7 @@ def tile_hybridattnresidualtransformerblock_kernel(tc, base, hidden, ln_gain, ln
             nc.scalar.activation(y_sb[:], y[:], ACT.Copy)
             nc.vector.tensor_tensor(windows[b][:].indirect(offsets[:]), x[:, b, :], y_sb[:], ADD)
             nc.sync.dma_start(out_blocks[:, b, :], windows[b][:])
-            if b == 1 or b == 3:
-                fill = SLAB + b // 2
-                nc.vector.tensor_copy(windows[fill][:], slabs[1][:, fill - SLAB, :])
             if b == SLAB - 1:
-                for fill in range(SLAB + 2, KB):
+                nc.vector.tensor_copy(windows[SLAB][:], slabs[1][:, 0, :])
+                for fill in range(SLAB + 1, KB):
                     nc.scalar.activation(windows[fill][:], slabs[1][:, fill - SLAB, :], ACT.Copy)

@@ -35,10 +35,10 @@ def tile_hybridattnresidualtransformerblock_kernel(tc, base, hidden, ln_gain, ln
         nc.sync.dma_start(offsets[:], offs)
         w1_sb = held.tile([P, KB, P, FB], BF16, name="w1_sb")
         nc.sync.dma_start(w1_sb[:], w1.rearrange("(p k) (m fb) -> p k m fb", k=KB, fb=FB))
-        slabs = [held.tile([P, SLAB, S], F32, name=f"slab{i}") for i in range(KB // SLAB)]
-        nc.sync.dma_start(slabs[0][:], base_blocks[:, 0:SLAB, :])
         w2_sb = held.tile([P, FB, P, KB], BF16, name="w2_sb")
         nc.sync.dma_start(w2_sb[:], w2.rearrange("(m fb) (q b) -> m fb q b", fb=FB, b=KB))
+        slabs = [held.tile([P, SLAB, S], F32, name=f"slab{i}") for i in range(KB // SLAB)]
+        nc.sync.dma_start(slabs[0][:], base_blocks[:, 0:SLAB, :])
         nc.sync.dma_start(slabs[1][:], base_blocks[:, SLAB:KB, :])
         windows = [held.tile([P, S], F32, name=f"window{b}") for b in range(KB)]
 
@@ -73,16 +73,37 @@ def tile_hybridattnresidualtransformerblock_kernel(tc, base, hidden, ln_gain, ln
             nc.tensor.matmul(spread[:], pick[:, a, :], eight, start=(a == 0), stop=(a == P // ROWS - 1))
         gain_bias = held.tile([P, 2, KB], F32, name="gain_bias")
         nc.vector.tensor_copy(gain_bias[:], spread[:])
-        centred = held.tile([P, KB, N], F32, name="centred")
-        squares = held.tile([P, KB, N], F32, name="squares")
+        shifted = held.tile([P, KB - 1, N], F32, name="shifted")
+        squares = held.tile([P, KB - 1, N], F32, name="squares")
+        for part in (slice(0, 4), slice(4, KB - 1)):
+            blocks = x[:, 1:KB, :][:, part, :]
+            first = x[:, 0, :].unsqueeze(1).to_broadcast([P, part.stop - part.start, N])
+            nc.vector.tensor_tensor(shifted[:, part, :], blocks, first, SUBTRACT)
+            nc.scalar.activation(squares[:, part, :], shifted[:, part, :], ACT.Square)
+        sum2 = held.tile([P, 2, N], F32, name="sum2")
+        nc.vector.tensor_tensor(sum2[:], sum4[:, 0:2, :], sum4[:, 2:4, :], ADD)
+        sum1 = held.tile([P, N], F32, name="sum1")
+        nc.vector.tensor_tensor(sum1[:], sum2[:, 0, :], sum2[:, 1, :], ADD)
+        partial = held.tile([P, N], F32, name="partial")
+        nc.vector.scalar_tensor_tensor(partial[:], x[:, 0, :], -4.0, sum1[:], op0=MULT, op1=ADD)
+        added = held.tile([P, 3, N], F32, name="added")
+        nc.vector.tensor_tensor(added[:], squares[:, 0:3, :], squares[:, 4:7, :], ADD)
         var = banks.tile([P, N], F32, name="var", tag="bank")
+        nc.tensor.matmul(var[:], averager[:], squares[:, 3, :], start=True, stop=False)
+        for i in range(3):
+            nc.tensor.matmul(var[:], averager[:], added[:, i, :], start=False, stop=False)
+        e = held.tile([P, N], F32, name="e")
+        nc.vector.tensor_tensor(e[:], x[:, 0, :], mean[:], SUBTRACT)
+        factor = held.tile([P, N], F32, name="factor")
+        nc.vector.scalar_tensor_tensor(factor[:], mean[:], -4.0, partial[:], op0=MULT, op1=ADD)
+        cross = held.tile([P, N], F32, name="cross")
+        nc.vector.scalar_tensor_tensor(cross[:], e[:], 2.0, factor[:], op0=MULT, op1=MULT)
+        nc.tensor.matmul(var[:], averager[:], cross[:], start=False, stop=True)
+        centred = held.tile([P, KB, N], F32, name="centred")
         mean_twice = mean[:].unsqueeze(1).to_broadcast([P, 2, N])
         for i in range(PAIRS):
             pair = slice(2 * i, 2 * i + 2)
             nc.vector.tensor_tensor(centred[:, pair, :], x[:, pair, :], mean_twice, SUBTRACT)
-            nc.scalar.activation(squares[:, pair, :], centred[:, pair, :], ACT.Square)
-            for k in range(2 * i, 2 * i + 2):
-                nc.tensor.matmul(var[:], averager[:], squares[:, k, :], start=(k == 0), stop=(k == KB - 1))
         rstd = held.tile([P, N], F32, name="rstd")
         nc.scalar.activation(rstd[:], var[:], ACT.Abs_reciprocal_sqrt, bias=eps[:])
 
@@ -100,8 +121,6 @@ def tile_hybridattnresidualtransformerblock_kernel(tc, base, hidden, ln_gain, ln
                     bias=gain_bias[:, 1, k : k + 1],
                     scale=gain_bias[:, 0, k : k + 1],
                 )
-        for b in range(SLAB):
-            nc.vector.tensor_copy(windows[b][:], slabs[0][:, b, :])
         act = held.tile([P, FB, N], BF16, name="act")
         h = [banks.tile([P, N], F32, name=f"h{fb}", tag="bank") for fb in range(FB)]
         for k in range(KB):
@@ -120,6 +139,9 @@ def tile_hybridattnresidualtransformerblock_kernel(tc, base, hidden, ln_gain, ln
                 nc.tensor.matmul(y[:], w2_sb[:, fb, :, b], act[:, fb, :], start=(fb == 0), stop=(fb == FB - 1))
             y_sb = ring.tile([P, N], F32, name="y_sb")
             nc.scalar.activation(y_sb[:], y[:], ACT.Copy)
+            if b < 2:
+                nc.vector.tensor_copy(windows[b][:], slabs[0][:, b, :])
+                nc.scalar.activation(windows[2 + b][:], slabs[0][:, 2 + b, :], ACT.Copy)
             nc.vector.tensor_tensor(windows[b][:].indirect(offsets[:]), x[:, b, :], y_sb[:], ADD)
             nc.sync.dma_start(out_blocks[:, b, :], windows[b][:])
             if b == SLAB - 1:

import concourse.mybir as mybir

P = 128
C, F, S, N = 1024, 1024, 1024, 128
KB = C // P
FB = F // P
PAIRS = KB // 2
ROWS = 32
SLAB = KB // 2
PSUM_BANKS = 8
LN_EPS = 1e-5
FLOPS = 2 * (2 * C * F * N)

F32, BF16, U16 = mybir.dt.float32, mybir.dt.bfloat16, mybir.dt.uint16
ADD, SUBTRACT, MULT = mybir.AluOpType.add, mybir.AluOpType.subtract, mybir.AluOpType.mult
ACT = mybir.ActivationFunctionType


def tile_hybridattnresidualtransformerblock_kernel(tc, base, hidden, ln_gain, ln_bias, w1, w2, offs, out):
    nc = tc.nc
    base_blocks = base.rearrange("(p k) s -> p k s", k=KB)
    out_blocks = out.rearrange("(p k) s -> p k s", k=KB)

    with (
        tc.tile_pool(name="held", bufs=1) as held,
        tc.tile_pool(name="ring", bufs=KB) as ring,
        tc.psum_pool(name="banks", bufs=PSUM_BANKS) as banks,
    ):
        x = held.tile([P, KB, N], F32, name="x")
        nc.sync.dma_start(x[:], hidden.rearrange("(p k) j -> p k j", k=KB))
        gain_bias_rows = held.tile([ROWS, 2, ROWS], F32, name="gain_bias_rows")
        nc.sync.dma_start(gain_bias_rows[:, 0, :], ln_gain.rearrange("(r i) o -> r (i o)", r=ROWS))
        nc.sync.dma_start(gain_bias_rows[:, 1, :], ln_bias.rearrange("(r i) o -> r (i o)", r=ROWS))
        offsets = held.tile([P, N // 16], U16, name="offsets")
        nc.sync.dma_start(offsets[:], offs)
        w1_sb = held.tile([P, KB, P, FB], BF16, name="w1_sb")
        nc.sync.dma_start(w1_sb[:], w1.rearrange("(p k) (m fb) -> p k m fb", k=KB, fb=FB))
        w2_sb = held.tile([P, FB, P, KB], BF16, name="w2_sb")
        nc.sync.dma_start(w2_sb[:], w2.rearrange("(m fb) (q b) -> m fb q b", fb=FB, b=KB))
        slabs = [held.tile([P, SLAB, S], F32, name=f"slab{i}") for i in range(KB // SLAB)]
        nc.sync.dma_start(slabs[0][:], base_blocks[:, 0:SLAB, :])
        nc.sync.dma_start(slabs[1][:], base_blocks[:, SLAB:KB, :])
        windows = [held.tile([P, S], F32, name=f"window{b}") for b in range(KB)]

        averager = held.tile([P, P], F32, name="averager")
        nc.vector.memset(averager[:], 1.0 / C)
        eps = held.tile([P, 1], F32, name="eps")
        nc.vector.memset(eps[:], LN_EPS)

        pick = held.tile([ROWS, P // ROWS, P], F32, name="pick")
        nc.gpsimd.memset(pick[:], 0.0)
        nc.gpsimd.affine_select(
            out=pick[:],
            in_=pick[:],
            compare_op=mybir.AluOpType.not_equal,
            fill=1.0,
            base=0,
            pattern=[[1, P // ROWS], [-1, P]],
            channel_multiplier=P // ROWS,
        )

        warm = held.tile([P, 1], F32, name="warm")
        nc.scalar.activation(warm[:], eps[:], ACT.Abs_reciprocal_sqrt)

        sum4 = held.tile([P, KB // 2, N], F32, name="sum4")
        nc.vector.tensor_tensor(sum4[:], x[:, 0 : KB // 2, :], x[:, KB // 2 : KB, :], ADD)
        mean = banks.tile([P, N], F32, name="mean", tag="bank")
        for i in range(KB // 2):
            nc.tensor.matmul(mean[:], averager[:], sum4[:, i, :], start=(i == 0), stop=(i == KB // 2 - 1))
        spread = banks.tile([P, 2, KB], F32, name="spread", tag="bank")
        for a in range(P // ROWS):
            eight = gain_bias_rows[:, :, KB * a : KB * (a + 1)]
            nc.tensor.matmul(spread[:], pick[:, a, :], eight, start=(a == 0), stop=(a == P // ROWS - 1))
        gain_bias = held.tile([P, 2, KB], F32, name="gain_bias")
        nc.vector.tensor_copy(gain_bias[:], spread[:])
        shifted = held.tile([P, KB - 1, N], F32, name="shifted")
        squares = held.tile([P, KB - 1, N], F32, name="squares")
        for part in (slice(0, 4), slice(4, KB - 1)):
            blocks = x[:, 1:KB, :][:, part, :]
            first = x[:, 0, :].unsqueeze(1).to_broadcast([P, part.stop - part.start, N])
            nc.vector.tensor_tensor(shifted[:, part, :], blocks, first, SUBTRACT)
            nc.scalar.activation(squares[:, part, :], shifted[:, part, :], ACT.Square)
        sum2 = held.tile([P, 2, N], F32, name="sum2")
        nc.vector.tensor_tensor(sum2[:], sum4[:, 0:2, :], sum4[:, 2:4, :], ADD)
        sum1 = held.tile([P, N], F32, name="sum1")
        nc.vector.tensor_tensor(sum1[:], sum2[:, 0, :], sum2[:, 1, :], ADD)
        partial = held.tile([P, N], F32, name="partial")
        nc.vector.scalar_tensor_tensor(partial[:], x[:, 0, :], -4.0, sum1[:], op0=MULT, op1=ADD)
        added = held.tile([P, 3, N], F32, name="added")
        nc.vector.tensor_tensor(added[:], squares[:, 0:3, :], squares[:, 4:7, :], ADD)
        var = banks.tile([P, N], F32, name="var", tag="bank")
        nc.tensor.matmul(var[:], averager[:], squares[:, 3, :], start=True, stop=False)
        for i in range(3):
            nc.tensor.matmul(var[:], averager[:], added[:, i, :], start=False, stop=False)
        e = held.tile([P, N], F32, name="e")
        nc.vector.tensor_tensor(e[:], x[:, 0, :], mean[:], SUBTRACT)
        factor = held.tile([P, N], F32, name="factor")
        nc.vector.scalar_tensor_tensor(factor[:], mean[:], -4.0, partial[:], op0=MULT, op1=ADD)
        cross = held.tile([P, N], F32, name="cross")
        nc.vector.scalar_tensor_tensor(cross[:], e[:], 2.0, factor[:], op0=MULT, op1=MULT)
        nc.tensor.matmul(var[:], averager[:], cross[:], start=False, stop=True)
        centred = held.tile([P, KB, N], F32, name="centred")
        mean_twice = mean[:].unsqueeze(1).to_broadcast([P, 2, N])
        for i in range(PAIRS):
            pair = slice(2 * i, 2 * i + 2)
            nc.vector.tensor_tensor(centred[:, pair, :], x[:, pair, :], mean_twice, SUBTRACT)
        rstd = held.tile([P, N], F32, name="rstd")
        nc.scalar.activation(rstd[:], var[:], ACT.Abs_reciprocal_sqrt, bias=eps[:])

        normed = held.tile([P, KB, N], F32, name="normed")
        xn = held.tile([P, KB, N], BF16, name="xn")
        rstd_twice = rstd[:].unsqueeze(1).to_broadcast([P, 2, N])
        for i in range(PAIRS):
            pair = slice(2 * i, 2 * i + 2)
            nc.vector.tensor_tensor(normed[:, pair, :], centred[:, pair, :], rstd_twice, MULT)
            for k in range(2 * i, 2 * i + 2):
                nc.scalar.activation(
                    xn[:, k, :],
                    normed[:, k, :],
                    ACT.Identity,
                    bias=gain_bias[:, 1, k : k + 1],
                    scale=gain_bias[:, 0, k : k + 1],
                )
        act = held.tile([P, FB, N], BF16, name="act")
        h = [banks.tile([P, N], F32, name=f"h{fb}", tag="bank") for fb in range(FB)]
        for k in range(KB):
            for fb in range(FB // 2):
                nc.tensor.matmul(h[fb][:], w1_sb[:, k, :, fb], xn[:, k, :], start=(k == 0), stop=(k == KB - 1))
        for fb in range(FB // 2):
            nc.scalar.activation(act[:, fb, :], h[fb][:], ACT.Gelu_apprx_tanh)
        for fb in range(FB // 2, FB):
            for k in range(KB):
                nc.tensor.matmul(h[fb][:], w1_sb[:, k, :, fb], xn[:, k, :], start=(k == 0), stop=(k == KB - 1))
            nc.scalar.activation(act[:, fb, :], h[fb][:], ACT.Gelu_apprx_tanh)

        for b in range(KB):
            y = banks.tile([P, N], F32, name="y", tag="bank")
            for fb in range(FB):
                nc.tensor.matmul(y[:], w2_sb[:, fb, :, b], act[:, fb, :], start=(fb == 0), stop=(fb == FB - 1))
            y_sb = ring.tile([P, N], F32, name="y_sb")
            nc.scalar.activation(y_sb[:], y[:], ACT.Copy)
            if b < 2:
                nc.vector.tensor_copy(windows[b][:], slabs[0][:, b, :])
                nc.scalar.activation(windows[2 + b][:], slabs[0][:, 2 + b, :], ACT.Copy)
            nc.vector.tensor_tensor(windows[b][:].indirect(offsets[:]), x[:, b, :], y_sb[:], ADD)
            nc.sync.dma_start(out_blocks[:, b, :], windows[b][:])
            if b == SLAB - 1:
                nc.vector.tensor_copy(windows[SLAB][:], slabs[1][:, 0, :])
                for fill in range(SLAB + 1, KB):
                    nc.scalar.activation(windows[fill][:], slabs[1][:, fill - SLAB, :], ACT.Copy)
